import numpy as np
import ml_dtypes


def mxq(x, axis, fmt="e4m3"):
    dtype, down = {"e4m3": (ml_dtypes.float8_e4m3fn, 7), "e5m2": (ml_dtypes.float8_e5m2, 14)}[fmt]
    v = np.moveaxis(np.asarray(x, np.float32).astype(ml_dtypes.bfloat16).astype(np.float64), axis, -1)
    blocks = v.reshape(v.shape[:-1] + (-1, 32))
    amax = np.abs(blocks).max(-1, keepdims=True)
    byte = np.maximum(np.where(amax > 0, np.frexp(amax)[1] - 1 + 127, 0) - down, 1)
    scale = np.exp2(byte - 127.0)
    codes = (blocks / scale).astype(np.float32).astype(dtype).astype(np.float64)
    return np.moveaxis((codes * scale).reshape(v.shape), -1, axis)


WIDE = False


def mx_kscale(k):
    if not WIDE:
        return np.ones(k)
    levels = np.array([30, -30])
    if k % 512:
        return np.exp2(np.random.permutation(np.resize(levels, k // 32))).repeat(32)
    a = np.empty((k // 512, 16))
    for p in range(k // 512):
        a[p, :8] = np.random.permutation(np.resize(levels, 8))
        for g in range(8):
            far = levels[np.abs(levels - a[p, g]) >= 10]
            a[p, g + 8] = far[np.random.randint(len(far))]
    return np.exp2(a.ravel()).repeat(32)


BF16 = ml_dtypes.bfloat16


def bf(x):
    return np.asarray(x, np.float32).astype(BF16)


def f64(x):
    return np.asarray(x).astype(np.float64)


B, L, DIM, H, D, QB = 1, 512, 2048, 16, 128, 512
HD = H * D
HALF = D // 2
EPS = 1e-6


def apply_rotary_emb(u, cos, sin):
    u1, u2 = u[..., :HALF], u[..., HALF:]
    return np.concatenate([u1 * cos + u2 * sin, u1 * -sin + u2 * cos], axis=-1)


def rms_norm(u):
    return u * (1.0 / np.sqrt(np.mean(u * u, axis=-1, keepdims=True) + EPS))


def setup_inputs():
    s = mx_kscale(DIM)
    inv_freq = 1.0 / (10000.0 ** (np.arange(HALF) / HALF))
    ang = np.arange(L)[:, None] * inv_freq[None, :]
    return {"x": bf(np.random.standard_normal((B, L, DIM)) * s),
            "cos": bf(np.cos(ang)[:, None, :]),
            "sin": bf(np.sin(ang)[:, None, :]),
            "Wq": bf(np.random.standard_normal((DIM, HD)) / np.sqrt(DIM) / s[:, None]),
            "Wk": bf(np.random.standard_normal((DIM, D)) / np.sqrt(DIM) / s[:, None]),
            "Wv": bf(np.random.standard_normal((DIM, D)) / np.sqrt(DIM) / s[:, None])}


def reference(x, cos, sin, Wq, Wk, Wv):
    xq = mxq(f64(x), 2, "e5m2")
    c, sn = f64(cos), f64(sin)
    q = (xq @ mxq(f64(Wq), 0, "e4m3")).reshape(B, L, H, D)
    k = xq @ mxq(f64(Wk), 0, "e4m3")
    v = xq @ mxq(f64(Wv), 0, "e4m3")
    q = rms_norm(apply_rotary_emb(q, c, sn))
    k = rms_norm(apply_rotary_emb(k[:, :, None, :], c, sn))[:, :, 0, :]
    return q, k, v

@@ -1,0 +1,260 @@
+from contextlib import ExitStack
+
+import concourse.mybir as mybir
+from concourse.masks import make_identity
+
+L, DIM, H, D = 512, 2048, 16, 128
+HALF = D // 2
+EPS = 1e-6
+FLOPS = 2 * L * DIM * (H * D + 2 * D)
+
+F32 = mybir.dt.float32
+BF16 = mybir.dt.bfloat16
+U32 = mybir.dt.uint32
+U8 = mybir.dt.uint8
+E4M3 = mybir.dt.float8_e4m3fn_x4
+E5M2 = mybir.dt.float8_e5m2_x4
+ACT = mybir.ActivationFunctionType
+ALU = mybir.AluOpType
+
+P = 128
+PACK = 4
+K_PASS = P * PACK
+PASSES = DIM // K_PASS
+TT = L // P
+CHUNKS = [256, 256, 512, 512, 512]
+V_COLS = 76
+NORMED = H + 1
+
+
+def tile_multiqueryattention_pa_kernel(tc, x, cos, sin, Wq, Wk, Wv, out_0, out_1, out_2):
+    nc = tc.nc
+    with ExitStack() as ctx:
+        keep = ctx.enter_context(tc.tile_pool(name="keep", bufs=1))
+        work = ctx.enter_context(tc.tile_pool(name="work", bufs=3))
+        outs = ctx.enter_context(tc.tile_pool(name="outs", bufs=10))
+        psum = ctx.enter_context(tc.psum_pool(name="psum", bufs=1))
+        ctx.enter_context(tc.manual_schedule())
+
+        x_rows = x[0].rearrange("(p t) k -> p t k", t=TT)
+        q_rows = out_0[0].rearrange("(p t) h d -> p t h d", t=TT)
+        k_rows = out_1[0].rearrange("(p t) d -> p t d", t=TT)
+        v_rows = out_2[0].rearrange("(p t) d -> p t d", t=TT)
+
+        cos_raw = keep.tile([P, TT, HALF], BF16, name="cos_raw")
+        sin_raw = keep.tile([P, TT, HALF], BF16, name="sin_raw")
+        nc.scalar.dma_start(out=cos_raw[:], in_=cos.rearrange("(p t) o j -> p t (o j)", t=TT))
+        nc.scalar.dma_start(out=sin_raw[:], in_=sin.rearrange("(p t) o j -> p t (o j)", t=TT))
+
+        x_raw = [keep.tile([P, TT, K_PASS], BF16, name="x_raw%d" % g) for g in range(PASSES)]
+        wk_raw = keep.tile([P, PASSES, PACK, D], BF16, name="wk_raw")
+        wv_raw = keep.tile([P, PASSES, PACK, D], BF16, name="wv_raw")
+        wq_raw = [keep.tile([P, PASSES, PACK, w], BF16, name="wq_raw%d" % c) for c, w in enumerate(CHUNKS)]
+
+        def load_x(g):
+            nc.sync.dma_start(out=x_raw[g][:], in_=x_rows[:, :, g * K_PASS : (g + 1) * K_PASS])
+
+        def load_narrow(raw, w_hbm):
+            nc.sync.dma_start(
+                out=raw[:].rearrange("p g j c -> p g (j c)"),
+                in_=w_hbm.rearrange("(g p j) c -> p g (j c)", g=PASSES, j=PACK),
+            )
+
+        load_x(0)
+        load_narrow(wk_raw, Wk)
+        load_x(1)
+        load_narrow(wv_raw, Wv)
+        load_x(2)
+        load_x(3)
+        head_raw = [wk_raw[:]]
+        col0 = 0
+        for c, w in enumerate(CHUNKS):
+            for g in range(PASSES):
+                rows = Wq[g * K_PASS : (g + 1) * K_PASS, col0 : col0 + w]
+                nc.sync.dma_start(out=wq_raw[c][:, g, :, :], in_=rows.rearrange("(p j) c -> p j c", j=PACK))
+            for i in range(w // D):
+                head_raw.append(wq_raw[c][:, :, :, i * D : (i + 1) * D])
+            col0 += w
+
+        ident = keep.tile([P, P], F32, name="ident")
+        make_identity(nc, ident[:])
+        swap = keep.tile([P, P], F32, name="swap")
+        nc.gpsimd.tensor_copy(out=swap[:, 0:HALF], in_=ident[:, HALF:D])
+        nc.gpsimd.tensor_copy(out=swap[:, HALF:D], in_=ident[:, 0:HALF])
+
+        rot_by_token = keep.tile([P, 2, TT, D], F32, name="rot_by_token")
+        rot = keep.tile([P, 2, L], F32, name="rot")
+
+        def build_rot_by_token():
+            nc.vector.tensor_copy(
+                out=rot_by_token[:, 0, :, :].rearrange("p t (e j) -> p t e j", e=2),
+                in_=cos_raw[:].unsqueeze(2).to_broadcast([P, TT, 2, HALF]),
+            )
+            nc.vector.tensor_scalar(
+                out=rot_by_token[:, 1, :, 0:HALF], in0=sin_raw[:], scalar1=-1.0, scalar2=None, op0=ALU.mult
+            )
+            nc.vector.tensor_copy(out=rot_by_token[:, 1, :, HALF:D], in_=sin_raw[:])
+
+        def transpose_rot():
+            for i in range(2):
+                bank = psum.tile([P, TT, P], F32, tag="turned", bufs=4, name="rot_bank")
+                for t in range(TT):
+                    nc.tensor.transpose(bank[:, t, :], rot_by_token[:, i, t, :], ident[:])
+                nc.scalar.activation(out=rot[:, i, :], in_=bank[:].rearrange("p t n -> p (t n)"), func=ACT.Copy)
+
+        x_codes = keep.tile([P, PASSES, L], U32, align_bytes=64, name="x_codes")
+        x_scales = keep.tile([P, PASSES, L], U8, align_bytes=64, name="x_scales")
+        x_grouped = {}
+
+        def transpose_x(g):
+            grouped = work.tile([P, L * PACK], BF16, align_bytes=64, tag="x_grouped", name="x_grouped")
+            x_grouped[g] = grouped
+            words_out = grouped[:].bitcast(F32).rearrange("p (t r u) -> p t r u", t=TT, u=2)
+            for t0 in range(0, TT, 2):
+                bank = psum.tile([P, 2, 2, P], F32, tag="turned", bufs=4, name="x_bank")
+                for t in range(2):
+                    words = x_raw[g][:, t0 + t, :].bitcast(F32)
+                    for u in range(2):
+                        nc.tensor.transpose(bank[:, t, u, :], words[:, u : 2 * P : 2], ident[:])
+                nc.scalar.copy(out=words_out[:, t0 : t0 + 2, :, :], in_=bank[:].rearrange("p t u r -> p t r u"))
+
+        def quantize_x(g):
+            nc.vector.quantize_mx(out=x_codes[:, g, :].bitcast(E5M2), scales=x_scales[:, g, :], in_=x_grouped[g][:])
+
+        w_grouped, w_codes, w_scales = {}, {}, {}
+
+        def interleave_w(name, raw, v_cols):
+            grouped = work.tile([P, PASSES, D, PACK], BF16, align_bytes=64, tag="w_grouped", name="w_grouped")
+            w_grouped[name] = grouped
+            src = raw.rearrange("p g j c -> p g c j")
+            nc.vector.tensor_copy(out=grouped[:, :, 0:v_cols, :], in_=src[:, :, 0:v_cols, :])
+            if v_cols < D:
+                nc.scalar.copy(out=grouped[:, :, v_cols:D, :], in_=src[:, :, v_cols:D, :])
+
+        def quantize_w(name):
+            codes = work.tile([P, PASSES * D], U32, align_bytes=64, tag="w_codes", bufs=4, name="w_codes")
+            scales = work.tile([P, PASSES * D], U8, align_bytes=64, tag="w_scales", bufs=4, name="w_scales")
+            w_codes[name], w_scales[name] = codes, scales
+            nc.vector.quantize_mx(
+                out=codes[:].bitcast(E4M3), scales=scales[:], in_=w_grouped[name][:].rearrange("p g c j -> p (g c j)")
+            )
+
+        proj = {}
+
+        def project_pass(s, g):
+            if g == 0:
+                proj[s] = psum.tile([P, L], F32, tag="proj", bufs=3, name="proj")
+            cols = slice(g * D, (g + 1) * D)
+            nc.tensor.matmul_mx(
+                out=proj[s][:],
+                lhsT=w_codes[s][:, cols].bitcast(E4M3),
+                lhsT_scale=w_scales[s][:, cols],
+                rhs=x_codes[:, g, :].bitcast(E5M2),
+                rhs_scale=x_scales[:, g, :],
+                start=(g == 0),
+                stop=(g == PASSES - 1),
+            )
+
+        v_bank = psum.tile([P, TT, D], F32, tag="v_bank", name="v_bank")
+
+        def value_pass(g):
+            cols = slice(g * D, (g + 1) * D)
+            for t in range(TT):
+                toks = slice(t * P, (t + 1) * P)
+                nc.tensor.matmul_mx(
+                    out=v_bank[:, t, :],
+                    lhsT=x_codes[:, g, toks].bitcast(E5M2),
+                    lhsT_scale=x_scales[:, g, toks],
+                    rhs=w_codes["v"][:, cols].bitcast(E4M3),
+                    rhs_scale=w_scales["v"][:, cols],
+                    start=(g == 0 and t == 0),
+                    stop=(g == PASSES - 1 and t == TT - 1),
+                )
+
+        terms, rotated, results, sum_sq, inv_rms = {}, {}, {}, {}, {}
+
+        def multiply_rot(s):
+            terms[s] = work.tile([P, 2, L], F32, tag="terms", name="terms")
+            nc.vector.tensor_tensor(
+                out=terms[s][:], in0=proj[s][:].unsqueeze(1).to_broadcast([P, 2, L]), in1=rot[:], op=ALU.mult
+            )
+
+        def turn_and_add(s):
+            rotated[s] = psum.tile([P, TT, D], F32, tag="turned", bufs=4, name="rotated")
+            for t in range(TT):
+                toks = slice(t * P, (t + 1) * P)
+                nc.tensor.matmul(
+                    rotated[s][:, t, :], lhsT=terms[s][:, 0, toks], rhs=ident[:], start=True, stop=False, is_transpose=True
+                )
+                nc.tensor.matmul(
+                    rotated[s][:, t, :], lhsT=terms[s][:, 1, toks], rhs=swap[:], start=False, stop=True, is_transpose=True
+                )
+
+        def sum_squares(s):
+            results[s] = outs.tile([P, TT, D], F32, tag="result", name="result")
+            sum_sq[s] = work.tile([P, TT], F32, tag="sum_sq", name="sum_sq")
+            for t in range(TT):
+                nc.scalar.activation(
+                    out=results[s][:, t, :], in_=rotated[s][:, t, :], func=ACT.Square, accum_out=sum_sq[s][:, t : t + 1]
+                )
+
+        def inverse_rms(s):
+            inv_rms[s] = work.tile([P, TT], F32, tag="inv_rms", name="inv_rms")
+            nc.scalar.activation(
+                out=inv_rms[s][:], in_=sum_sq[s][:], func=ACT.Abs_reciprocal_sqrt, scale=1.0 / D, bias=EPS
+            )
+
+        def scale_and_store(s):
+            for t in range(TT):
+                nc.scalar.activation(
+                    out=results[s][:, t, :], in_=rotated[s][:, t, :], func=ACT.Copy, scale=inv_rms[s][:, t : t + 1]
+                )
+            nc.sync.dma_start(out=k_rows if s == 0 else q_rows[:, :, s - 1, :], in_=results[s][:])
+
+        def store_values():
+            result = outs.tile([P, TT, D], F32, tag="result", name="result")
+            nc.scalar.copy(out=result[:], in_=v_bank[:])
+            nc.sync.dma_start(out=v_rows, in_=result[:])
+
+        build_rot_by_token()
+        transpose_x(0)
+        interleave_w(0, head_raw[0], D)
+        quantize_x(0)
+        quantize_w(0)
+        transpose_x(1)
+        interleave_w("v", wv_raw[:], D)
+        quantize_x(1)
+        quantize_w("v")
+        for g in range(2, PASSES):
+            project_pass(0, g - 2)
+            value_pass(g - 2)
+            transpose_x(g)
+            quantize_x(g)
+        project_pass(0, 2)
+        value_pass(2)
+        transpose_rot()
+        project_pass(0, 3)
+        value_pass(3)
+        interleave_w(1, head_raw[1], V_COLS)
+        interleave_w(2, head_raw[2], V_COLS)
+        quantize_w(1)
+        store_values()
+
+        for s in range(NORMED + 2):
+            if s < NORMED:
+                multiply_rot(s)
+            if s + 2 < NORMED:
+                quantize_w(s + 2)
+            if s + 3 < NORMED:
+                interleave_w(s + 3, head_raw[s + 3], V_COLS)
+            if 1 <= s <= NORMED:
+                turn_and_add(s - 1)
+            if s + 1 < NORMED:
+                for g in range(PASSES):
+                    project_pass(s + 1, g)
+            if 1 <= s <= NORMED:
+                sum_squares(s - 1)
+            if s >= 2:
+                scale_and_store(s - 2)
+            if 1 <= s <= NORMED:
+                inverse_rms(s - 1)

@@ -23,8 +23,10 @@ K_PASS = P * PACK
 PASSES = DIM // K_PASS
 TT = L // P
 CHUNKS = [256, 256, 512, 512, 512]
-V_COLS = 76
+VECTOR_COLS = 84
 NORMED = H + 1
+VALUE = NORMED
+VECTOR_SCALED = 3
 
 
 def tile_multiqueryattention_pa_kernel(tc, x, cos, sin, Wq, Wk, Wv, out_0, out_1, out_2):
@@ -47,34 +49,27 @@ def tile_multiqueryattention_pa_kernel(tc, x, cos, sin, Wq, Wk, Wv, out_0, out_1
         nc.scalar.dma_start(out=sin_raw[:], in_=sin.rearrange("(p t) o j -> p t (o j)", t=TT))
 
         x_raw = [keep.tile([P, TT, K_PASS], BF16, name="x_raw%d" % g) for g in range(PASSES)]
-        wk_raw = keep.tile([P, PASSES, PACK, D], BF16, name="wk_raw")
-        wv_raw = keep.tile([P, PASSES, PACK, D], BF16, name="wv_raw")
-        wq_raw = [keep.tile([P, PASSES, PACK, w], BF16, name="wq_raw%d" % c) for c, w in enumerate(CHUNKS)]
-
-        def load_x(g):
+        for g in range(PASSES):
             nc.sync.dma_start(out=x_raw[g][:], in_=x_rows[:, :, g * K_PASS : (g + 1) * K_PASS])
 
-        def load_narrow(raw, w_hbm):
+        def load_one_head(name, w_hbm):
+            raw = keep.tile([P, PASSES, PACK, D], BF16, name=name)
             nc.sync.dma_start(
                 out=raw[:].rearrange("p g j c -> p g (j c)"),
                 in_=w_hbm.rearrange("(g p j) c -> p g (j c)", g=PASSES, j=PACK),
             )
+            return raw[:]
 
-        load_x(0)
-        load_narrow(wk_raw, Wk)
-        load_x(1)
-        load_narrow(wv_raw, Wv)
-        load_x(2)
-        load_x(3)
-        head_raw = [wk_raw[:]]
+        w_raw = [load_one_head("wk_raw", Wk)]
         col0 = 0
-        for c, w in enumerate(CHUNKS):
+        for c, width in enumerate(CHUNKS):
+            raw = keep.tile([P, PASSES, PACK, width], BF16, name="wq_raw%d" % c)
             for g in range(PASSES):
-                rows = Wq[g * K_PASS : (g + 1) * K_PASS, col0 : col0 + w]
-                nc.sync.dma_start(out=wq_raw[c][:, g, :, :], in_=rows.rearrange("(p j) c -> p j c", j=PACK))
-            for i in range(w // D):
-                head_raw.append(wq_raw[c][:, :, :, i * D : (i + 1) * D])
-            col0 += w
+                rows = Wq[g * K_PASS : (g + 1) * K_PASS, col0 : col0 + width]
+                nc.sync.dma_start(out=raw[:, g, :, :], in_=rows.rearrange("(p j) c -> p j c", j=PACK))
+            w_raw.extend(raw[:, :, :, i * D : (i + 1) * D] for i in range(width // D))
+            col0 += width
+        w_raw.append(load_one_head("wv_raw", Wv))
 
         ident = keep.tile([P, P], F32, name="ident")
         make_identity(nc, ident[:])
@@ -82,40 +77,42 @@ def tile_multiqueryattention_pa_kernel(tc, x, cos, sin, Wq, Wk, Wv, out_0, out_1
         nc.gpsimd.tensor_copy(out=swap[:, 0:HALF], in_=ident[:, HALF:D])
         nc.gpsimd.tensor_copy(out=swap[:, HALF:D], in_=ident[:, 0:HALF])
 
-        rot_by_token = keep.tile([P, 2, TT, D], F32, name="rot_by_token")
         rot = keep.tile([P, 2, L], F32, name="rot")
 
-        def build_rot_by_token():
+        def build_rot():
+            by_token = keep.tile([P, 2, TT, D], F32, name="rot_by_token")
             nc.vector.tensor_copy(
-                out=rot_by_token[:, 0, :, :].rearrange("p t (e j) -> p t e j", e=2),
+                out=by_token[:, 0, :, :].rearrange("p t (e j) -> p t e j", e=2),
                 in_=cos_raw[:].unsqueeze(2).to_broadcast([P, TT, 2, HALF]),
             )
             nc.vector.tensor_scalar(
-                out=rot_by_token[:, 1, :, 0:HALF], in0=sin_raw[:], scalar1=-1.0, scalar2=None, op0=ALU.mult
+                out=by_token[:, 1, :, 0:HALF], in0=sin_raw[:], scalar1=-1.0, scalar2=None, op0=ALU.mult
             )
-            nc.vector.tensor_copy(out=rot_by_token[:, 1, :, HALF:D], in_=sin_raw[:])
-
-        def transpose_rot():
+            nc.vector.tensor_copy(out=by_token[:, 1, :, HALF:D], in_=sin_raw[:])
             for i in range(2):
                 bank = psum.tile([P, TT, P], F32, tag="turned", bufs=4, name="rot_bank")
                 for t in range(TT):
-                    nc.tensor.transpose(bank[:, t, :], rot_by_token[:, i, t, :], ident[:])
+                    nc.tensor.transpose(bank[:, t, :], by_token[:, i, t, :], ident[:])
                 nc.scalar.activation(out=rot[:, i, :], in_=bank[:].rearrange("p t n -> p (t n)"), func=ACT.Copy)
 
         x_codes = keep.tile([P, PASSES, L], U32, align_bytes=64, name="x_codes")
         x_scales = keep.tile([P, PASSES, L], U8, align_bytes=64, name="x_scales")
-        x_grouped = {}
+        x_split, x_grouped = {}, {}
+
+        def split_x(g):
+            x_split[g] = work.tile([P, TT, 2, P], F32, tag="x_split", name="x_split")
+            nc.vector.tensor_copy(
+                out=x_split[g][:], in_=x_raw[g][:].bitcast(F32).rearrange("p t (w u) -> p t u w", u=2)
+            )
 
         def transpose_x(g):
-            grouped = work.tile([P, L * PACK], BF16, align_bytes=64, tag="x_grouped", name="x_grouped")
-            x_grouped[g] = grouped
-            words_out = grouped[:].bitcast(F32).rearrange("p (t r u) -> p t r u", t=TT, u=2)
+            x_grouped[g] = work.tile([P, L * PACK], BF16, align_bytes=64, tag="x_grouped", name="x_grouped")
+            words_out = x_grouped[g][:].bitcast(F32).rearrange("p (t r u) -> p t r u", t=TT, u=2)
             for t0 in range(0, TT, 2):
                 bank = psum.tile([P, 2, 2, P], F32, tag="turned", bufs=4, name="x_bank")
                 for t in range(2):
-                    words = x_raw[g][:, t0 + t, :].bitcast(F32)
                     for u in range(2):
-                        nc.tensor.transpose(bank[:, t, u, :], words[:, u : 2 * P : 2], ident[:])
+                        nc.tensor.transpose(bank[:, t, u, :], x_split[g][:, t0 + t, u, :], ident[:])
                 nc.scalar.copy(out=words_out[:, t0 : t0 + 2, :, :], in_=bank[:].rearrange("p t u r -> p t r u"))
 
         def quantize_x(g):
@@ -123,138 +120,146 @@ def tile_multiqueryattention_pa_kernel(tc, x, cos, sin, Wq, Wk, Wv, out_0, out_1
 
         w_grouped, w_codes, w_scales = {}, {}, {}
 
-        def interleave_w(name, raw, v_cols):
-            grouped = work.tile([P, PASSES, D, PACK], BF16, align_bytes=64, tag="w_grouped", name="w_grouped")
-            w_grouped[name] = grouped
-            src = raw.rearrange("p g j c -> p g c j")
-            nc.vector.tensor_copy(out=grouped[:, :, 0:v_cols, :], in_=src[:, :, 0:v_cols, :])
-            if v_cols < D:
-                nc.scalar.copy(out=grouped[:, :, v_cols:D, :], in_=src[:, :, v_cols:D, :])
+        def interleave_w(h, vector_cols):
+            w_grouped[h] = work.tile([P, PASSES, D, PACK], BF16, align_bytes=64, tag="w_grouped", name="w_grouped")
+            dst = w_grouped[h][:].rearrange("p g (c i) j -> p g c j i", i=4)
+            src = w_raw[h].rearrange("p g j (c i) -> p g c j i", i=4)
+            cut = vector_cols // 4
+            nc.vector.tensor_copy(out=dst[:, :, 0:cut, :, :], in_=src[:, :, 0:cut, :, :])
+            if vector_cols < D:
+                nc.scalar.copy(out=dst[:, :, cut : D // 4, :, :], in_=src[:, :, cut : D // 4, :, :])
 
-        def quantize_w(name):
-            codes = work.tile([P, PASSES * D], U32, align_bytes=64, tag="w_codes", bufs=4, name="w_codes")
-            scales = work.tile([P, PASSES * D], U8, align_bytes=64, tag="w_scales", bufs=4, name="w_scales")
-            w_codes[name], w_scales[name] = codes, scales
+        def quantize_w(h):
+            w_codes[h] = work.tile([P, PASSES * D], U32, align_bytes=64, tag="w_codes", bufs=4, name="w_codes")
+            w_scales[h] = work.tile([P, PASSES * D], U8, align_bytes=64, tag="w_scales", bufs=4, name="w_scales")
             nc.vector.quantize_mx(
-                out=codes[:].bitcast(E4M3), scales=scales[:], in_=w_grouped[name][:].rearrange("p g c j -> p (g c j)")
+                out=w_codes[h][:].bitcast(E4M3),
+                scales=w_scales[h][:],
+                in_=w_grouped[h][:].rearrange("p g c j -> p (g c j)"),
             )
 
-        proj = {}
+        proj, terms, rotated, results, sum_sq, inv_rms = {}, {}, {}, {}, {}, {}
 
-        def project_pass(s, g):
-            if g == 0:
-                proj[s] = psum.tile([P, L], F32, tag="proj", bufs=3, name="proj")
-            cols = slice(g * D, (g + 1) * D)
-            nc.tensor.matmul_mx(
-                out=proj[s][:],
-                lhsT=w_codes[s][:, cols].bitcast(E4M3),
-                lhsT_scale=w_scales[s][:, cols],
-                rhs=x_codes[:, g, :].bitcast(E5M2),
-                rhs_scale=x_scales[:, g, :],
-                start=(g == 0),
-                stop=(g == PASSES - 1),
-            )
+        def project(h):
+            proj[h] = psum.tile([P, L], F32, tag="proj", bufs=3, name="proj")
+            for g in range(PASSES):
+                cols = slice(g * D, (g + 1) * D)
+                nc.tensor.matmul_mx(
+                    out=proj[h][:],
+                    lhsT=w_codes[h][:, cols].bitcast(E4M3),
+                    lhsT_scale=w_scales[h][:, cols],
+                    rhs=x_codes[:, g, :].bitcast(E5M2),
+                    rhs_scale=x_scales[:, g, :],
+                    start=(g == 0),
+                    stop=(g == PASSES - 1),
+                )
 
         v_bank = psum.tile([P, TT, D], F32, tag="v_bank", name="v_bank")
 
-        def value_pass(g):
-            cols = slice(g * D, (g + 1) * D)
-            for t in range(TT):
-                toks = slice(t * P, (t + 1) * P)
+        def project_values(t):
+            toks = slice(t * P, (t + 1) * P)
+            for g in range(PASSES):
+                cols = slice(g * D, (g + 1) * D)
                 nc.tensor.matmul_mx(
                     out=v_bank[:, t, :],
                     lhsT=x_codes[:, g, toks].bitcast(E5M2),
                     lhsT_scale=x_scales[:, g, toks],
-                    rhs=w_codes["v"][:, cols].bitcast(E4M3),
-                    rhs_scale=w_scales["v"][:, cols],
-                    start=(g == 0 and t == 0),
-                    stop=(g == PASSES - 1 and t == TT - 1),
+                    rhs=w_codes[VALUE][:, cols].bitcast(E4M3),
+                    rhs_scale=w_scales[VALUE][:, cols],
+                    start=(g == 0),
+                    stop=(g == PASSES - 1),
                 )
 
-        terms, rotated, results, sum_sq, inv_rms = {}, {}, {}, {}, {}
-
-        def multiply_rot(s):
-            terms[s] = work.tile([P, 2, L], F32, tag="terms", name="terms")
+        def multiply_rot(h):
+            terms[h] = work.tile([P, 2, L], F32, tag="terms", name="terms")
             nc.vector.tensor_tensor(
-                out=terms[s][:], in0=proj[s][:].unsqueeze(1).to_broadcast([P, 2, L]), in1=rot[:], op=ALU.mult
+                out=terms[h][:],
+                in0=proj[h][:].unsqueeze(1).to_broadcast([P, 2, L]),
+                in1=rot[:],
+                op=ALU.mult,
             )
 
-        def turn_and_add(s):
-            rotated[s] = psum.tile([P, TT, D], F32, tag="turned", bufs=4, name="rotated")
+        def turn_and_add(h):
+            rotated[h] = psum.tile([P, TT, D], F32, tag="turned", bufs=4, name="rotated")
             for t in range(TT):
                 toks = slice(t * P, (t + 1) * P)
                 nc.tensor.matmul(
-                    rotated[s][:, t, :], lhsT=terms[s][:, 0, toks], rhs=ident[:], start=True, stop=False, is_transpose=True
+                    rotated[h][:, t, :], lhsT=terms[h][:, 0, toks], rhs=ident[:], start=True, stop=False, is_transpose=True
                 )
                 nc.tensor.matmul(
-                    rotated[s][:, t, :], lhsT=terms[s][:, 1, toks], rhs=swap[:], start=False, stop=True, is_transpose=True
+                    rotated[h][:, t, :], lhsT=terms[h][:, 1, toks], rhs=swap[:], start=False, stop=True, is_transpose=True
                 )
 
-        def sum_squares(s):
-            results[s] = outs.tile([P, TT, D], F32, tag="result", name="result")
-            sum_sq[s] = work.tile([P, TT], F32, tag="sum_sq", name="sum_sq")
+        def sum_squares(h):
+            results[h] = outs.tile([P, TT, D], F32, tag="result", name="result")
+            sum_sq[h] = work.tile([P, TT], F32, tag="sum_sq", name="sum_sq")
             for t in range(TT):
                 nc.scalar.activation(
-                    out=results[s][:, t, :], in_=rotated[s][:, t, :], func=ACT.Square, accum_out=sum_sq[s][:, t : t + 1]
+                    out=results[h][:, t, :], in_=rotated[h][:, t, :], func=ACT.Square, accum_out=sum_sq[h][:, t : t + 1]
                 )
 
-        def inverse_rms(s):
-            inv_rms[s] = work.tile([P, TT], F32, tag="inv_rms", name="inv_rms")
+        def inverse_rms(h):
+            inv_rms[h] = work.tile([P, TT], F32, tag="inv_rms", name="inv_rms")
             nc.scalar.activation(
-                out=inv_rms[s][:], in_=sum_sq[s][:], func=ACT.Abs_reciprocal_sqrt, scale=1.0 / D, bias=EPS
+                out=inv_rms[h][:], in_=sum_sq[h][:], func=ACT.Abs_reciprocal_sqrt, scale=1.0 / D, bias=EPS
             )
 
-        def scale_and_store(s):
-            for t in range(TT):
-                nc.scalar.activation(
-                    out=results[s][:, t, :], in_=rotated[s][:, t, :], func=ACT.Copy, scale=inv_rms[s][:, t : t + 1]
+        def scale_and_store(h):
+            if h >= NORMED - VECTOR_SCALED:
+                nc.vector.tensor_tensor(
+                    out=results[h][:],
+                    in0=rotated[h][:],
+                    in1=inv_rms[h][:].unsqueeze(2).to_broadcast([P, TT, D]),
+                    op=ALU.mult,
                 )
-            nc.sync.dma_start(out=k_rows if s == 0 else q_rows[:, :, s - 1, :], in_=results[s][:])
+            else:
+                for t in range(TT):
+                    nc.scalar.activation(
+                        out=results[h][:, t, :], in_=rotated[h][:, t, :], func=ACT.Copy, scale=inv_rms[h][:, t : t + 1]
+                    )
+            nc.sync.dma_start(out=k_rows if h == 0 else q_rows[:, :, h - 1, :], in_=results[h][:])
 
         def store_values():
             result = outs.tile([P, TT, D], F32, tag="result", name="result")
-            nc.scalar.copy(out=result[:], in_=v_bank[:])
+            nc.vector.tensor_copy(out=result[:], in_=v_bank[:])
             nc.sync.dma_start(out=v_rows, in_=result[:])
 
-        build_rot_by_token()
-        transpose_x(0)
-        interleave_w(0, head_raw[0], D)
-        quantize_x(0)
-        quantize_w(0)
-        transpose_x(1)
-        interleave_w("v", wv_raw[:], D)
-        quantize_x(1)
-        quantize_w("v")
-        for g in range(2, PASSES):
-            project_pass(0, g - 2)
-            value_pass(g - 2)
+        build_rot()
+        split_x(0)
+        for g in range(PASSES):
             transpose_x(g)
-            quantize_x(g)
-        project_pass(0, 2)
-        value_pass(2)
-        transpose_rot()
-        project_pass(0, 3)
-        value_pass(3)
-        interleave_w(1, head_raw[1], V_COLS)
-        interleave_w(2, head_raw[2], V_COLS)
+            if g + 1 < PASSES:
+                split_x(g + 1)
+            if 1 <= g < PASSES - 1:
+                quantize_x(g - 1)
+        interleave_w(0, D)
+        quantize_x(PASSES - 2)
+        quantize_w(0)
+        quantize_x(PASSES - 1)
+        project(0)
+        interleave_w(1, VECTOR_COLS)
+        interleave_w(2, VECTOR_COLS)
         quantize_w(1)
-        store_values()
 
         for s in range(NORMED + 2):
             if s < NORMED:
                 multiply_rot(s)
-            if s + 2 < NORMED:
+            if s + 2 <= VALUE:
                 quantize_w(s + 2)
-            if s + 3 < NORMED:
-                interleave_w(s + 3, head_raw[s + 3], V_COLS)
+            if s + 3 <= VALUE:
+                interleave_w(s + 3, VECTOR_COLS)
             if 1 <= s <= NORMED:
                 turn_and_add(s - 1)
             if s + 1 < NORMED:
-                for g in range(PASSES):
-                    project_pass(s + 1, g)
+                project(s + 1)
+            if NORMED - 1 <= s <= NORMED:
+                for t in range(TT // 2):
+                    project_values((s - NORMED + 1) * (TT // 2) + t)
             if 1 <= s <= NORMED:
                 sum_squares(s - 1)
             if s >= 2:
                 scale_and_store(s - 2)
+            if s == NORMED:
+                store_values()
             if 1 <= s <= NORMED:
                 inverse_rms(s - 1)

@@ -23,7 +23,6 @@ K_PASS = P * PACK
 PASSES = DIM // K_PASS
 TT = L // P
 CHUNKS = [256, 256, 512, 512, 512]
-VECTOR_COLS = 84
 NORMED = H + 1
 VALUE = NORMED
 VECTOR_SCALED = 3
@@ -43,15 +42,13 @@ def tile_multiqueryattention_pa_kernel(tc, x, cos, sin, Wq, Wk, Wv, out_0, out_1
         k_rows = out_1[0].rearrange("(p t) d -> p t d", t=TT)
         v_rows = out_2[0].rearrange("(p t) d -> p t d", t=TT)
 
+        def x_pieces(g):
+            return [slice(0, TT // 2), slice(TT // 2, TT)] if g == 0 else [slice(0, TT)]
+
         cos_raw = keep.tile([P, TT, HALF], BF16, name="cos_raw")
         sin_raw = keep.tile([P, TT, HALF], BF16, name="sin_raw")
-        nc.scalar.dma_start(out=cos_raw[:], in_=cos.rearrange("(p t) o j -> p t (o j)", t=TT))
-        nc.scalar.dma_start(out=sin_raw[:], in_=sin.rearrange("(p t) o j -> p t (o j)", t=TT))
 
         x_raw = [keep.tile([P, TT, K_PASS], BF16, name="x_raw%d" % g) for g in range(PASSES)]
-        for g in range(PASSES):
-            nc.sync.dma_start(out=x_raw[g][:], in_=x_rows[:, :, g * K_PASS : (g + 1) * K_PASS])
-
         def load_one_head(name, w_hbm):
             raw = keep.tile([P, PASSES, PACK, D], BF16, name=name)
             nc.sync.dma_start(
@@ -60,6 +57,12 @@ def tile_multiqueryattention_pa_kernel(tc, x, cos, sin, Wq, Wk, Wv, out_0, out_1
             )
             return raw[:]
 
+        for g in range(PASSES):
+            for toks in x_pieces(g):
+                nc.sync.dma_start(out=x_raw[g][:, toks, :], in_=x_rows[:, toks, g * K_PASS : (g + 1) * K_PASS])
+            if g == 0:
+                nc.sync.dma_start(out=cos_raw[:], in_=cos.rearrange("(p t) o j -> p t (o j)", t=TT))
+                nc.sync.dma_start(out=sin_raw[:], in_=sin.rearrange("(p t) o j -> p t (o j)", t=TT))
         w_raw = [load_one_head("wk_raw", Wk)]
         col0 = 0
         for c, width in enumerate(CHUNKS):
@@ -77,23 +80,25 @@ def tile_multiqueryattention_pa_kernel(tc, x, cos, sin, Wq, Wk, Wv, out_0, out_1
         nc.gpsimd.tensor_copy(out=swap[:, 0:HALF], in_=ident[:, HALF:D])
         nc.gpsimd.tensor_copy(out=swap[:, HALF:D], in_=ident[:, 0:HALF])
 
-        rot = keep.tile([P, 2, L], F32, name="rot")
+        ident_bf16 = keep.tile([P, P], BF16, name="ident_bf16")
+        make_identity(nc, ident_bf16[:])
+        rot_by_token = keep.tile([P, 2, TT, D], BF16, name="rot_by_token")
+        rot = keep.tile([P, 2, L], BF16, name="rot")
 
-        def build_rot():
-            by_token = keep.tile([P, 2, TT, D], F32, name="rot_by_token")
-            nc.vector.tensor_copy(
-                out=by_token[:, 0, :, :].rearrange("p t (e j) -> p t e j", e=2),
+        def lay_out_rot():
+            nc.scalar.activation(out=rot_by_token[:, 1, :, 0:HALF], in_=sin_raw[:], func=ACT.Copy, scale=-1.0)
+            nc.scalar.copy(out=rot_by_token[:, 1, :, HALF:D], in_=sin_raw[:])
+            nc.scalar.copy(
+                out=rot_by_token[:, 0, :, :].rearrange("p t (e j) -> p t e j", e=2),
                 in_=cos_raw[:].unsqueeze(2).to_broadcast([P, TT, 2, HALF]),
             )
-            nc.vector.tensor_scalar(
-                out=by_token[:, 1, :, 0:HALF], in0=sin_raw[:], scalar1=-1.0, scalar2=None, op0=ALU.mult
-            )
-            nc.vector.tensor_copy(out=by_token[:, 1, :, HALF:D], in_=sin_raw[:])
+
+        def transpose_rot():
+            bank = psum.tile([P, 2, TT, P], BF16, tag="turned", bufs=4, name="rot_bank")
             for i in range(2):
-                bank = psum.tile([P, TT, P], F32, tag="turned", bufs=4, name="rot_bank")
                 for t in range(TT):
-                    nc.tensor.transpose(bank[:, t, :], by_token[:, i, t, :], ident[:])
-                nc.scalar.activation(out=rot[:, i, :], in_=bank[:].rearrange("p t n -> p (t n)"), func=ACT.Copy)
+                    nc.tensor.transpose(bank[:, i, t, :], rot_by_token[:, i, t, :], ident_bf16[:])
+            nc.scalar.copy(out=rot[:], in_=bank[:].rearrange("p i t n -> p i (t n)"))
 
         x_codes = keep.tile([P, PASSES, L], U32, align_bytes=64, name="x_codes")
         x_scales = keep.tile([P, PASSES, L], U8, align_bytes=64, name="x_scales")
@@ -101,9 +106,11 @@ def tile_multiqueryattention_pa_kernel(tc, x, cos, sin, Wq, Wk, Wv, out_0, out_1
 
         def split_x(g):
             x_split[g] = work.tile([P, TT, 2, P], F32, tag="x_split", name="x_split")
-            nc.vector.tensor_copy(
-                out=x_split[g][:], in_=x_raw[g][:].bitcast(F32).rearrange("p t (w u) -> p t u w", u=2)
-            )
+            for toks in x_pieces(g):
+                nc.vector.tensor_copy(
+                    out=x_split[g][:, toks, :, :],
+                    in_=x_raw[g][:, toks, :].bitcast(F32).rearrange("p t (w u) -> p t u w", u=2),
+                )
 
         def transpose_x(g):
             x_grouped[g] = work.tile([P, L * PACK], BF16, align_bytes=64, tag="x_grouped", name="x_grouped")
@@ -118,23 +125,37 @@ def tile_multiqueryattention_pa_kernel(tc, x, cos, sin, Wq, Wk, Wv, out_0, out_1
         def quantize_x(g):
             nc.vector.quantize_mx(out=x_codes[:, g, :].bitcast(E5M2), scales=x_scales[:, g, :], in_=x_grouped[g][:])
 
-        w_grouped, w_codes, w_scales = {}, {}, {}
+        w_grouped, w_last, w_codes, w_scales = {}, {}, {}, {}
 
-        def interleave_w(h, vector_cols):
-            w_grouped[h] = work.tile([P, PASSES, D, PACK], BF16, align_bytes=64, tag="w_grouped", name="w_grouped")
-            dst = w_grouped[h][:].rearrange("p g (c i) j -> p g c j i", i=4)
-            src = w_raw[h].rearrange("p g j (c i) -> p g c j i", i=4)
-            cut = vector_cols // 4
-            nc.vector.tensor_copy(out=dst[:, :, 0:cut, :, :], in_=src[:, :, 0:cut, :, :])
-            if vector_cols < D:
-                nc.scalar.copy(out=dst[:, :, cut : D // 4, :, :], in_=src[:, :, cut : D // 4, :, :])
+        def interleave(copy, dst, src):
+            copy(out=dst.rearrange("p g (c i) j -> p g c j i", i=4), in_=src.rearrange("p g j (c i) -> p g c j i", i=4))
+
+        def interleave_w(h, third_copy):
+            w_grouped[h] = work.tile([P, PASSES - 1, D, PACK], BF16, align_bytes=64, tag="w_grouped", name="w_grouped")
+            interleave(nc.vector.tensor_copy, w_grouped[h][:, 0:2, :, :], w_raw[h][:, 0:2, :, :])
+            interleave(third_copy, w_grouped[h][:, 2:3, :, :], w_raw[h][:, 2:3, :, :])
+
+        def interleave_last(h, engine):
+            w_last[h] = work.tile([P, D, PACK], BF16, align_bytes=64, tag="w_last", bufs=1, name="w_last")
+            if engine == "gpsimd":
+                nc.gpsimd.tensor_copy(out=w_last[h][:], in_=w_raw[h][:, PASSES - 1, :, :].rearrange("p j c -> p c j"))
+            else:
+                copy = nc.vector.tensor_copy if engine == "vector" else nc.scalar.copy
+                interleave(copy, w_last[h][:].unsqueeze(1), w_raw[h][:, PASSES - 1 : PASSES, :, :])
+
+        def quantize_last(h):
+            cols = slice((PASSES - 1) * D, PASSES * D)
+            nc.vector.quantize_mx(
+                out=w_codes[h][:, cols].bitcast(E4M3), scales=w_scales[h][:, cols], in_=w_last[h][:].rearrange("p c j -> p (c j)")
+            )
 
         def quantize_w(h):
             w_codes[h] = work.tile([P, PASSES * D], U32, align_bytes=64, tag="w_codes", bufs=4, name="w_codes")
             w_scales[h] = work.tile([P, PASSES * D], U8, align_bytes=64, tag="w_scales", bufs=4, name="w_scales")
+            cols = slice(0, (PASSES - 1) * D)
             nc.vector.quantize_mx(
-                out=w_codes[h][:].bitcast(E4M3),
-                scales=w_scales[h][:],
+                out=w_codes[h][:, cols].bitcast(E4M3),
+                scales=w_scales[h][:, cols],
                 in_=w_grouped[h][:].rearrange("p g c j -> p (g c j)"),
             )
 
@@ -224,7 +245,7 @@ def tile_multiqueryattention_pa_kernel(tc, x, cos, sin, Wq, Wk, Wv, out_0, out_1
             nc.vector.tensor_copy(out=result[:], in_=v_bank[:])
             nc.sync.dma_start(out=v_rows, in_=result[:])
 
-        build_rot()
+        lay_out_rot()
         split_x(0)
         for g in range(PASSES):
             transpose_x(g)
@@ -232,22 +253,30 @@ def tile_multiqueryattention_pa_kernel(tc, x, cos, sin, Wq, Wk, Wv, out_0, out_1
                 split_x(g + 1)
             if 1 <= g < PASSES - 1:
                 quantize_x(g - 1)
-        interleave_w(0, D)
+        transpose_rot()
+        interleave_last(0, "vector")
+        interleave_w(0, nc.vector.tensor_copy)
         quantize_x(PASSES - 2)
         quantize_w(0)
+        quantize_last(0)
         quantize_x(PASSES - 1)
         project(0)
-        interleave_w(1, VECTOR_COLS)
-        interleave_w(2, VECTOR_COLS)
+        interleave_last(1, "scalar")
+        interleave_w(1, nc.scalar.copy)
+        interleave_w(2, nc.scalar.copy)
         quantize_w(1)
+        quantize_last(1)
+        interleave_last(2, "scalar")
 
         for s in range(NORMED + 2):
             if s < NORMED:
                 multiply_rot(s)
             if s + 2 <= VALUE:
                 quantize_w(s + 2)
+                quantize_last(s + 2)
             if s + 3 <= VALUE:
-                interleave_w(s + 3, VECTOR_COLS)
+                interleave_w(s + 3, nc.scalar.copy)
+                interleave_last(s + 3, "gpsimd")
             if 1 <= s <= NORMED:
                 turn_and_add(s - 1)
             if s + 1 < NORMED:

@@ -22,10 +22,14 @@ PACK = 4
 K_PASS = P * PACK
 PASSES = DIM // K_PASS
 TT = L // P
-CHUNKS = [256, 256, 512, 512, 512]
-NORMED = H + 1
-VALUE = NORMED
-VECTOR_SCALED = 3
+LAST = H
+VALUE = H + 1
+PAIR = PASSES // 2
+RUN = 4
+WQ_WIDTHS = [256, 256, 512, 512, 512]
+VECTOR_TILES = 3
+ALL_TILES = (0, TT)
+FIRST_TILES, SECOND_TILES = (0, TT // 2), (TT // 2, TT // 2)
 
 
 def tile_multiqueryattention_pa_kernel(tc, x, cos, sin, Wq, Wk, Wv, out_0, out_1, out_2):
@@ -37,6 +41,12 @@ def tile_multiqueryattention_pa_kernel(tc, x, cos, sin, Wq, Wk, Wv, out_0, out_1
         psum = ctx.enter_context(tc.psum_pool(name="psum", bufs=1))
         ctx.enter_context(tc.manual_schedule())
 
+        def product_bank(shape):
+            return psum.tile(shape, F32, tag="product", bufs=3, name="product")
+
+        def transpose_bank(shape, dtype):
+            return psum.tile(shape, dtype, tag="transposed", bufs=5, name="transposed")
+
         x_rows = x[0].rearrange("(p t) k -> p t k", t=TT)
         q_rows = out_0[0].rearrange("(p t) h d -> p t h d", t=TT)
         k_rows = out_1[0].rearrange("(p t) d -> p t d", t=TT)
@@ -45,10 +55,6 @@ def tile_multiqueryattention_pa_kernel(tc, x, cos, sin, Wq, Wk, Wv, out_0, out_1
         def x_pieces(g):
             return [slice(0, TT // 2), slice(TT // 2, TT)] if g == 0 else [slice(0, TT)]
 
-        cos_raw = keep.tile([P, TT, HALF], BF16, name="cos_raw")
-        sin_raw = keep.tile([P, TT, HALF], BF16, name="sin_raw")
-
-        x_raw = [keep.tile([P, TT, K_PASS], BF16, name="x_raw%d" % g) for g in range(PASSES)]
         def load_one_head(name, w_hbm):
             raw = keep.tile([P, PASSES, PACK, D], BF16, name=name)
             nc.sync.dma_start(
@@ -57,16 +63,20 @@ def tile_multiqueryattention_pa_kernel(tc, x, cos, sin, Wq, Wk, Wv, out_0, out_1
             )
             return raw[:]
 
+        cos_raw = keep.tile([P, TT, HALF], BF16, name="cos_raw")
+        sin_raw = keep.tile([P, TT, HALF], BF16, name="sin_raw")
+        x_raw = [keep.tile([P, TT, K_PASS], BF16, name="x_raw%d" % g) for g in range(PASSES)]
         for g in range(PASSES):
             for toks in x_pieces(g):
                 nc.sync.dma_start(out=x_raw[g][:, toks, :], in_=x_rows[:, toks, g * K_PASS : (g + 1) * K_PASS])
             if g == 0:
                 nc.sync.dma_start(out=cos_raw[:], in_=cos.rearrange("(p t) o j -> p t (o j)", t=TT))
                 nc.sync.dma_start(out=sin_raw[:], in_=sin.rearrange("(p t) o j -> p t (o j)", t=TT))
+
         w_raw = [load_one_head("wk_raw", Wk)]
         col0 = 0
-        for c, width in enumerate(CHUNKS):
-            raw = keep.tile([P, PASSES, PACK, width], BF16, name="wq_raw%d" % c)
+        for n, width in enumerate(WQ_WIDTHS):
+            raw = keep.tile([P, PASSES, PACK, width], BF16, name="wq_raw%d" % n)
             for g in range(PASSES):
                 rows = Wq[g * K_PASS : (g + 1) * K_PASS, col0 : col0 + width]
                 nc.sync.dma_start(out=raw[:, g, :, :], in_=rows.rearrange("(p j) c -> p j c", j=PACK))
@@ -79,9 +89,9 @@ def tile_multiqueryattention_pa_kernel(tc, x, cos, sin, Wq, Wk, Wv, out_0, out_1
         swap = keep.tile([P, P], F32, name="swap")
         nc.gpsimd.tensor_copy(out=swap[:, 0:HALF], in_=ident[:, HALF:D])
         nc.gpsimd.tensor_copy(out=swap[:, HALF:D], in_=ident[:, 0:HALF])
-
         ident_bf16 = keep.tile([P, P], BF16, name="ident_bf16")
         make_identity(nc, ident_bf16[:])
+
         rot_by_token = keep.tile([P, 2, TT, D], BF16, name="rot_by_token")
         rot = keep.tile([P, 2, L], BF16, name="rot")
 
@@ -94,7 +104,7 @@ def tile_multiqueryattention_pa_kernel(tc, x, cos, sin, Wq, Wk, Wv, out_0, out_1
             )
 
         def transpose_rot():
-            bank = psum.tile([P, 2, TT, P], BF16, tag="turned", bufs=4, name="rot_bank")
+            bank = transpose_bank([P, 2, TT, P], BF16)
             for i in range(2):
                 for t in range(TT):
                     nc.tensor.transpose(bank[:, i, t, :], rot_by_token[:, i, t, :], ident_bf16[:])
@@ -116,7 +126,7 @@ def tile_multiqueryattention_pa_kernel(tc, x, cos, sin, Wq, Wk, Wv, out_0, out_1
             x_grouped[g] = work.tile([P, L * PACK], BF16, align_bytes=64, tag="x_grouped", name="x_grouped")
             words_out = x_grouped[g][:].bitcast(F32).rearrange("p (t r u) -> p t r u", t=TT, u=2)
             for t0 in range(0, TT, 2):
-                bank = psum.tile([P, 2, 2, P], F32, tag="turned", bufs=4, name="x_bank")
+                bank = transpose_bank([P, 2, 2, P], F32)
                 for t in range(2):
                     for u in range(2):
                         nc.tensor.transpose(bank[:, t, u, :], x_split[g][:, t0 + t, u, :], ident[:])
@@ -125,44 +135,40 @@ def tile_multiqueryattention_pa_kernel(tc, x, cos, sin, Wq, Wk, Wv, out_0, out_1
         def quantize_x(g):
             nc.vector.quantize_mx(out=x_codes[:, g, :].bitcast(E5M2), scales=x_scales[:, g, :], in_=x_grouped[g][:])
 
-        w_grouped, w_last, w_codes, w_scales = {}, {}, {}, {}
+        w_grouped, w_codes, w_scales = {}, {}, {}
 
-        def interleave(copy, dst, src):
-            copy(out=dst.rearrange("p g (c i) j -> p g c j i", i=4), in_=src.rearrange("p g j (c i) -> p g c j i", i=4))
+        def grouped_tile(h, half):
+            w_grouped[h, half] = work.tile(
+                [P, PAIR, D, PACK], BF16, align_bytes=64, tag="w_grouped%d" % half, bufs=3 - half, name="w_grouped"
+            )
+            return w_grouped[h, half][:], w_raw[h][:, PAIR * half : PAIR * (half + 1), :, :]
 
-        def interleave_w(h, third_copy):
-            w_grouped[h] = work.tile([P, PASSES - 1, D, PACK], BF16, align_bytes=64, tag="w_grouped", name="w_grouped")
-            interleave(nc.vector.tensor_copy, w_grouped[h][:, 0:2, :, :], w_raw[h][:, 0:2, :, :])
-            interleave(third_copy, w_grouped[h][:, 2:3, :, :], w_raw[h][:, 2:3, :, :])
-
-        def interleave_last(h, engine):
-            w_last[h] = work.tile([P, D, PACK], BF16, align_bytes=64, tag="w_last", bufs=1, name="w_last")
-            if engine == "gpsimd":
-                nc.gpsimd.tensor_copy(out=w_last[h][:], in_=w_raw[h][:, PASSES - 1, :, :].rearrange("p j c -> p c j"))
-            else:
-                copy = nc.vector.tensor_copy if engine == "vector" else nc.scalar.copy
-                interleave(copy, w_last[h][:].unsqueeze(1), w_raw[h][:, PASSES - 1 : PASSES, :, :])
-
-        def quantize_last(h):
-            cols = slice((PASSES - 1) * D, PASSES * D)
-            nc.vector.quantize_mx(
-                out=w_codes[h][:, cols].bitcast(E4M3), scales=w_scales[h][:, cols], in_=w_last[h][:].rearrange("p c j -> p (c j)")
+        def interleave_w(h, half, copy):
+            grouped, raw = grouped_tile(h, half)
+            copy(
+                out=grouped.rearrange("p g (c i) j -> p g c j i", i=RUN),
+                in_=raw.rearrange("p g j (c i) -> p g c j i", i=RUN),
             )
 
-        def quantize_w(h):
-            w_codes[h] = work.tile([P, PASSES * D], U32, align_bytes=64, tag="w_codes", bufs=4, name="w_codes")
-            w_scales[h] = work.tile([P, PASSES * D], U8, align_bytes=64, tag="w_scales", bufs=4, name="w_scales")
-            cols = slice(0, (PASSES - 1) * D)
+        def interleave_w_on_gpsimd(h):
+            grouped, raw = grouped_tile(h, 1)
+            nc.gpsimd.tensor_copy(out=grouped, in_=raw.rearrange("p g j c -> p g c j"))
+
+        def quantize_w(h, half):
+            if h not in w_codes:
+                w_codes[h] = work.tile([P, PASSES * D], U32, align_bytes=64, tag="w_codes", bufs=4, name="w_codes")
+                w_scales[h] = work.tile([P, PASSES * D], U8, align_bytes=64, tag="w_scales", bufs=4, name="w_scales")
+            cols = slice(PAIR * half * D, PAIR * (half + 1) * D)
             nc.vector.quantize_mx(
                 out=w_codes[h][:, cols].bitcast(E4M3),
                 scales=w_scales[h][:, cols],
-                in_=w_grouped[h][:].rearrange("p g c j -> p (g c j)"),
+                in_=w_grouped[h, half][:].rearrange("p g c j -> p (g c j)"),
             )
 
-        proj, terms, rotated, results, sum_sq, inv_rms = {}, {}, {}, {}, {}, {}
+        proj, terms, rotated, results, sum_sq, inv_rms, values = {}, {}, {}, {}, {}, {}, {}
 
         def project(h):
-            proj[h] = psum.tile([P, L], F32, tag="proj", bufs=3, name="proj")
+            proj[h] = product_bank([P, L])
             for g in range(PASSES):
                 cols = slice(g * D, (g + 1) * D)
                 nc.tensor.matmul_mx(
@@ -175,75 +181,97 @@ def tile_multiqueryattention_pa_kernel(tc, x, cos, sin, Wq, Wk, Wv, out_0, out_1
                     stop=(g == PASSES - 1),
                 )
 
-        v_bank = psum.tile([P, TT, D], F32, tag="v_bank", name="v_bank")
-
-        def project_values(t):
-            toks = slice(t * P, (t + 1) * P)
-            for g in range(PASSES):
-                cols = slice(g * D, (g + 1) * D)
-                nc.tensor.matmul_mx(
-                    out=v_bank[:, t, :],
-                    lhsT=x_codes[:, g, toks].bitcast(E5M2),
-                    lhsT_scale=x_scales[:, g, toks],
-                    rhs=w_codes[VALUE][:, cols].bitcast(E4M3),
-                    rhs_scale=w_scales[VALUE][:, cols],
-                    start=(g == 0),
-                    stop=(g == PASSES - 1),
-                )
-
-        def multiply_rot(h):
-            terms[h] = work.tile([P, 2, L], F32, tag="terms", name="terms")
+        def multiply_rot(h, part=ALL_TILES):
+            t0, nt = part
+            toks = slice(t0 * P, (t0 + nt) * P)
+            terms[h, part] = work.tile([P, 2, nt * P], F32, tag="terms", name="terms")
             nc.vector.tensor_tensor(
-                out=terms[h][:],
-                in0=proj[h][:].unsqueeze(1).to_broadcast([P, 2, L]),
-                in1=rot[:],
+                out=terms[h, part][:],
+                in0=proj[h][:, toks].unsqueeze(1).to_broadcast([P, 2, nt * P]),
+                in1=rot[:, :, toks],
                 op=ALU.mult,
             )
 
-        def turn_and_add(h):
-            rotated[h] = psum.tile([P, TT, D], F32, tag="turned", bufs=4, name="rotated")
-            for t in range(TT):
-                toks = slice(t * P, (t + 1) * P)
-                nc.tensor.matmul(
-                    rotated[h][:, t, :], lhsT=terms[h][:, 0, toks], rhs=ident[:], start=True, stop=False, is_transpose=True
-                )
-                nc.tensor.matmul(
-                    rotated[h][:, t, :], lhsT=terms[h][:, 1, toks], rhs=swap[:], start=False, stop=True, is_transpose=True
-                )
+        def transpose_and_add(h, part=ALL_TILES):
+            nt = part[1]
+            rotated[h, part] = transpose_bank([P, nt, D], F32)
+            for t in range(nt):
+                for i, permutation in enumerate((ident, swap)):
+                    nc.tensor.matmul(
+                        rotated[h, part][:, t, :],
+                        lhsT=terms[h, part][:, i, t * P : (t + 1) * P],
+                        rhs=permutation[:],
+                        start=(i == 0),
+                        stop=(i == 1),
+                        is_transpose=True,
+                    )
 
-        def sum_squares(h):
-            results[h] = outs.tile([P, TT, D], F32, tag="result", name="result")
-            sum_sq[h] = work.tile([P, TT], F32, tag="sum_sq", name="sum_sq")
-            for t in range(TT):
+        def sum_squares(h, part=ALL_TILES):
+            nt = part[1]
+            results[h, part] = outs.tile([P, nt, D], F32, tag="result", name="result")
+            sum_sq[h, part] = work.tile([P, nt], F32, tag="sum_sq", name="sum_sq")
+            for t in range(nt):
                 nc.scalar.activation(
-                    out=results[h][:, t, :], in_=rotated[h][:, t, :], func=ACT.Square, accum_out=sum_sq[h][:, t : t + 1]
+                    out=results[h, part][:, t, :],
+                    in_=rotated[h, part][:, t, :],
+                    func=ACT.Square,
+                    accum_out=sum_sq[h, part][:, t : t + 1],
                 )
 
-        def inverse_rms(h):
-            inv_rms[h] = work.tile([P, TT], F32, tag="inv_rms", name="inv_rms")
+        def inverse_rms(h, part=ALL_TILES):
+            inv_rms[h, part] = work.tile([P, part[1]], F32, tag="inv_rms", name="inv_rms")
             nc.scalar.activation(
-                out=inv_rms[h][:], in_=sum_sq[h][:], func=ACT.Abs_reciprocal_sqrt, scale=1.0 / D, bias=EPS
+                out=inv_rms[h, part][:], in_=sum_sq[h, part][:], func=ACT.Abs_reciprocal_sqrt, scale=1.0 / D, bias=EPS
             )
 
-        def scale_and_store(h):
-            if h >= NORMED - VECTOR_SCALED:
-                nc.vector.tensor_tensor(
-                    out=results[h][:],
-                    in0=rotated[h][:],
-                    in1=inv_rms[h][:].unsqueeze(2).to_broadcast([P, TT, D]),
-                    op=ALU.mult,
-                )
-            else:
-                for t in range(TT):
-                    nc.scalar.activation(
-                        out=results[h][:, t, :], in_=rotated[h][:, t, :], func=ACT.Copy, scale=inv_rms[h][:, t : t + 1]
-                    )
-            nc.sync.dma_start(out=k_rows if h == 0 else q_rows[:, :, h - 1, :], in_=results[h][:])
+        def scale_on_vector(h, part, count):
+            nc.vector.tensor_tensor(
+                out=results[h, part][:, 0:count, :],
+                in0=rotated[h, part][:, 0:count, :],
+                in1=inv_rms[h, part][:, 0:count].unsqueeze(2).to_broadcast([P, count, D]),
+                op=ALU.mult,
+            )
 
-        def store_values():
-            result = outs.tile([P, TT, D], F32, tag="result", name="result")
-            nc.vector.tensor_copy(out=result[:], in_=v_bank[:])
-            nc.sync.dma_start(out=v_rows, in_=result[:])
+        def scale_on_scalar(h, part, first):
+            for t in range(first, part[1]):
+                nc.scalar.activation(
+                    out=results[h, part][:, t, :],
+                    in_=rotated[h, part][:, t, :],
+                    func=ACT.Copy,
+                    scale=inv_rms[h, part][:, t : t + 1],
+                )
+
+        def store(h, part=ALL_TILES):
+            t0, nt = part
+            rows = k_rows if h == 0 else q_rows[:, :, h - 1, :]
+            nc.sync.dma_start(out=rows[:, t0 : t0 + nt, :], in_=results[h, part][:])
+
+        def scale_on_vector_and_store(h, part=ALL_TILES):
+            scale_on_vector(h, part, part[1])
+            store(h, part)
+
+        def project_values(part):
+            t0, nt = part
+            values[part] = product_bank([P, nt, D])
+            for t in range(nt):
+                toks = slice((t0 + t) * P, (t0 + t + 1) * P)
+                for g in range(PASSES):
+                    cols = slice(g * D, (g + 1) * D)
+                    nc.tensor.matmul_mx(
+                        out=values[part][:, t, :],
+                        lhsT=x_codes[:, g, toks].bitcast(E5M2),
+                        lhsT_scale=x_scales[:, g, toks],
+                        rhs=w_codes[VALUE][:, cols].bitcast(E4M3),
+                        rhs_scale=w_scales[VALUE][:, cols],
+                        start=(g == 0),
+                        stop=(g == PASSES - 1),
+                    )
+
+        def store_values(part):
+            t0, nt = part
+            result = outs.tile([P, nt, D], F32, tag="result", name="result")
+            nc.vector.tensor_copy(out=result[:], in_=values[part][:])
+            nc.sync.dma_start(out=v_rows[:, t0 : t0 + nt, :], in_=result[:])
 
         lay_out_rot()
         split_x(0)
@@ -254,41 +282,69 @@ def tile_multiqueryattention_pa_kernel(tc, x, cos, sin, Wq, Wk, Wv, out_0, out_1
             if 1 <= g < PASSES - 1:
                 quantize_x(g - 1)
         transpose_rot()
-        interleave_last(0, "vector")
-        interleave_w(0, nc.vector.tensor_copy)
+        interleave_w(0, 0, nc.vector.tensor_copy)
+        interleave_w(0, 1, nc.vector.tensor_copy)
         quantize_x(PASSES - 2)
-        quantize_w(0)
-        quantize_last(0)
+        quantize_w(0, 0)
+        quantize_w(0, 1)
         quantize_x(PASSES - 1)
         project(0)
-        interleave_last(1, "scalar")
-        interleave_w(1, nc.scalar.copy)
-        interleave_w(2, nc.scalar.copy)
-        quantize_w(1)
-        quantize_last(1)
-        interleave_last(2, "scalar")
+        interleave_w(1, 0, nc.scalar.copy)
+        interleave_w(1, 1, nc.vector.tensor_copy)
+        interleave_w(2, 0, nc.scalar.copy)
+        interleave_w(2, 1, nc.scalar.copy)
+        quantize_w(1, 1)
+        quantize_w(1, 0)
+        interleave_w_on_gpsimd(3)
 
-        for s in range(NORMED + 2):
-            if s < NORMED:
-                multiply_rot(s)
-            if s + 2 <= VALUE:
-                quantize_w(s + 2)
-                quantize_last(s + 2)
-            if s + 3 <= VALUE:
-                interleave_w(s + 3, nc.scalar.copy)
-                interleave_last(s + 3, "gpsimd")
-            if 1 <= s <= NORMED:
-                turn_and_add(s - 1)
-            if s + 1 < NORMED:
-                project(s + 1)
-            if NORMED - 1 <= s <= NORMED:
-                for t in range(TT // 2):
-                    project_values((s - NORMED + 1) * (TT // 2) + t)
-            if 1 <= s <= NORMED:
-                sum_squares(s - 1)
+        for s in range(LAST - 1):
+            multiply_rot(s)
             if s >= 2:
-                scale_and_store(s - 2)
-            if s == NORMED:
-                store_values()
-            if 1 <= s <= NORMED:
+                scale_on_vector(s - 2, ALL_TILES, VECTOR_TILES)
+            quantize_w(s + 2, 1)
+            quantize_w(s + 2, 0)
+            if s + 4 <= VALUE:
+                interleave_w_on_gpsimd(s + 4)
+            if s >= 1:
+                transpose_and_add(s - 1)
+            project(s + 1)
+            if s >= 1:
+                sum_squares(s - 1)
+            interleave_w(s + 3, 0, nc.scalar.copy)
+            if s >= 2:
+                scale_on_scalar(s - 2, ALL_TILES, VECTOR_TILES)
+                store(s - 2)
+            if s >= 1:
                 inverse_rms(s - 1)
+
+        halves = (FIRST_TILES, SECOND_TILES)
+        multiply_rot(LAST - 1)
+        quantize_w(VALUE, 1)
+        quantize_w(VALUE, 0)
+        transpose_and_add(LAST - 2)
+        project(LAST)
+        sum_squares(LAST - 2)
+        scale_on_scalar(LAST - 3, ALL_TILES, 0)
+        store(LAST - 3)
+        inverse_rms(LAST - 2)
+
+        for part in halves:
+            multiply_rot(LAST, part)
+        transpose_and_add(LAST - 1)
+        project_values(FIRST_TILES)
+        for part in halves:
+            transpose_and_add(LAST, part)
+        project_values(SECOND_TILES)
+        sum_squares(LAST - 1)
+        scale_on_vector_and_store(LAST - 2)
+        inverse_rms(LAST - 1)
+
+        for part in halves:
+            sum_squares(LAST, part)
+        for part in halves:
+            inverse_rms(LAST, part)
+        store_values(FIRST_TILES)
+        scale_on_vector_and_store(LAST - 1)
+        store_values(SECOND_TILES)
+        for part in halves:
+            scale_on_vector_and_store(LAST, part)

@@ -24,10 +24,9 @@ PASSES = DIM // K_PASS
 TT = L // P
 LAST = H
 VALUE = H + 1
-PAIR = PASSES // 2
 RUN = 4
 WQ_WIDTHS = [256, 256, 512, 512, 512]
-VECTOR_TILES = 3
+VECTOR_COLS = 108
 ALL_TILES = (0, TT)
 FIRST_TILES, SECOND_TILES = (0, TT // 2), (TT // 2, TT // 2)
 
@@ -135,35 +134,41 @@ def tile_multiqueryattention_pa_kernel(tc, x, cos, sin, Wq, Wk, Wv, out_0, out_1
         def quantize_x(g):
             nc.vector.quantize_mx(out=x_codes[:, g, :].bitcast(E5M2), scales=x_scales[:, g, :], in_=x_grouped[g][:])
 
-        w_grouped, w_codes, w_scales = {}, {}, {}
+        w_front, w_last, w_codes, w_scales = {}, {}, {}, {}
 
-        def grouped_tile(h, half):
-            w_grouped[h, half] = work.tile(
-                [P, PAIR, D, PACK], BF16, align_bytes=64, tag="w_grouped%d" % half, bufs=3 - half, name="w_grouped"
-            )
-            return w_grouped[h, half][:], w_raw[h][:, PAIR * half : PAIR * (half + 1), :, :]
-
-        def interleave_w(h, half, copy):
-            grouped, raw = grouped_tile(h, half)
-            copy(
+        def interleave_on_vector(grouped, raw):
+            nc.vector.tensor_copy(
                 out=grouped.rearrange("p g (c i) j -> p g c j i", i=RUN),
                 in_=raw.rearrange("p g j (c i) -> p g c j i", i=RUN),
             )
 
-        def interleave_w_on_gpsimd(h):
-            grouped, raw = grouped_tile(h, 1)
-            nc.gpsimd.tensor_copy(out=grouped, in_=raw.rearrange("p g j c -> p g c j"))
+        def interleave_on_scalar(grouped, raw):
+            nc.scalar.copy(out=grouped, in_=raw.rearrange("p g j c -> p g c j"))
 
-        def quantize_w(h, half):
-            if h not in w_codes:
-                w_codes[h] = work.tile([P, PASSES * D], U32, align_bytes=64, tag="w_codes", bufs=4, name="w_codes")
-                w_scales[h] = work.tile([P, PASSES * D], U8, align_bytes=64, tag="w_scales", bufs=4, name="w_scales")
-            cols = slice(PAIR * half * D, PAIR * (half + 1) * D)
-            nc.vector.quantize_mx(
-                out=w_codes[h][:, cols].bitcast(E4M3),
-                scales=w_scales[h][:, cols],
-                in_=w_grouped[h, half][:].rearrange("p g c j -> p (g c j)"),
-            )
+        def interleave_on_gpsimd(grouped, raw):
+            nc.gpsimd.tensor_copy(out=grouped[:, 0, :, :], in_=raw[:, 0, :, :].rearrange("p j c -> p c j"))
+
+        def interleave_front(h, vector_cols, interleave_third):
+            w_front[h] = work.tile([P, PASSES - 1, D, PACK], BF16, align_bytes=64, tag="w_front", name="w_front")
+            interleave_on_vector(w_front[h][:, 0:2, 0:vector_cols, :], w_raw[h][:, 0:2, :, 0:vector_cols])
+            interleave_third(w_front[h][:, 2:3, :, :], w_raw[h][:, 2:3, :, :])
+            if vector_cols < D:
+                interleave_on_scalar(w_front[h][:, 0:2, vector_cols:D, :], w_raw[h][:, 0:2, :, vector_cols:D])
+
+        def interleave_last(h, interleave):
+            w_last[h] = work.tile([P, 1, D, PACK], BF16, align_bytes=64, tag="w_last", bufs=1, name="w_last")
+            interleave(w_last[h][:], w_raw[h][:, PASSES - 1 : PASSES, :, :])
+
+        def quantize_w(h):
+            w_codes[h] = work.tile([P, PASSES * D], U32, align_bytes=64, tag="w_codes", bufs=4, name="w_codes")
+            w_scales[h] = work.tile([P, PASSES * D], U8, align_bytes=64, tag="w_scales", bufs=4, name="w_scales")
+            cut = (PASSES - 1) * D
+            for grouped, cols in ((w_front[h], slice(0, cut)), (w_last[h], slice(cut, PASSES * D))):
+                nc.vector.quantize_mx(
+                    out=w_codes[h][:, cols].bitcast(E4M3),
+                    scales=w_scales[h][:, cols],
+                    in_=grouped[:].rearrange("p g c j -> p (g c j)"),
+                )
 
         proj, terms, rotated, results, sum_sq, inv_rms, values = {}, {}, {}, {}, {}, {}, {}
 
@@ -224,30 +229,28 @@ def tile_multiqueryattention_pa_kernel(tc, x, cos, sin, Wq, Wk, Wv, out_0, out_1
                 out=inv_rms[h, part][:], in_=sum_sq[h, part][:], func=ACT.Abs_reciprocal_sqrt, scale=1.0 / D, bias=EPS
             )
 
-        def scale_on_vector(h, part, count):
-            nc.vector.tensor_tensor(
-                out=results[h, part][:, 0:count, :],
-                in0=rotated[h, part][:, 0:count, :],
-                in1=inv_rms[h, part][:, 0:count].unsqueeze(2).to_broadcast([P, count, D]),
-                op=ALU.mult,
-            )
-
-        def scale_on_scalar(h, part, first):
-            for t in range(first, part[1]):
-                nc.scalar.activation(
-                    out=results[h, part][:, t, :],
-                    in_=rotated[h, part][:, t, :],
-                    func=ACT.Copy,
-                    scale=inv_rms[h, part][:, t : t + 1],
-                )
-
-        def store(h, part=ALL_TILES):
+        def store(h, part):
             t0, nt = part
             rows = k_rows if h == 0 else q_rows[:, :, h - 1, :]
             nc.sync.dma_start(out=rows[:, t0 : t0 + nt, :], in_=results[h, part][:])
 
+        def scale_on_scalar_and_store(h):
+            for t in range(TT):
+                nc.scalar.activation(
+                    out=results[h, ALL_TILES][:, t, :],
+                    in_=rotated[h, ALL_TILES][:, t, :],
+                    func=ACT.Copy,
+                    scale=inv_rms[h, ALL_TILES][:, t : t + 1],
+                )
+            store(h, ALL_TILES)
+
         def scale_on_vector_and_store(h, part=ALL_TILES):
-            scale_on_vector(h, part, part[1])
+            nc.vector.tensor_tensor(
+                out=results[h, part][:],
+                in0=rotated[h, part][:],
+                in1=inv_rms[h, part][:].unsqueeze(2).to_broadcast([P, part[1], D]),
+                op=ALU.mult,
+            )
             store(h, part)
 
         def project_values(part):
@@ -282,50 +285,40 @@ def tile_multiqueryattention_pa_kernel(tc, x, cos, sin, Wq, Wk, Wv, out_0, out_1
             if 1 <= g < PASSES - 1:
                 quantize_x(g - 1)
         transpose_rot()
-        interleave_w(0, 0, nc.vector.tensor_copy)
-        interleave_w(0, 1, nc.vector.tensor_copy)
+        interleave_last(0, interleave_on_vector)
+        interleave_front(0, D, interleave_on_vector)
         quantize_x(PASSES - 2)
-        quantize_w(0, 0)
-        quantize_w(0, 1)
+        quantize_w(0)
         quantize_x(PASSES - 1)
         project(0)
-        interleave_w(1, 0, nc.scalar.copy)
-        interleave_w(1, 1, nc.vector.tensor_copy)
-        interleave_w(2, 0, nc.scalar.copy)
-        interleave_w(2, 1, nc.scalar.copy)
-        quantize_w(1, 1)
-        quantize_w(1, 0)
-        interleave_w_on_gpsimd(3)
+        interleave_last(1, interleave_on_scalar)
+        interleave_front(1, VECTOR_COLS, interleave_on_scalar)
+        interleave_front(2, VECTOR_COLS, interleave_on_scalar)
+        quantize_w(1)
+        interleave_last(2, interleave_on_scalar)
 
         for s in range(LAST - 1):
             multiply_rot(s)
-            if s >= 2:
-                scale_on_vector(s - 2, ALL_TILES, VECTOR_TILES)
-            quantize_w(s + 2, 1)
-            quantize_w(s + 2, 0)
-            if s + 4 <= VALUE:
-                interleave_w_on_gpsimd(s + 4)
+            quantize_w(s + 2)
+            interleave_front(s + 3, VECTOR_COLS, interleave_on_scalar)
+            interleave_last(s + 3, interleave_on_gpsimd)
             if s >= 1:
                 transpose_and_add(s - 1)
             project(s + 1)
             if s >= 1:
                 sum_squares(s - 1)
-            interleave_w(s + 3, 0, nc.scalar.copy)
             if s >= 2:
-                scale_on_scalar(s - 2, ALL_TILES, VECTOR_TILES)
-                store(s - 2)
+                scale_on_scalar_and_store(s - 2)
             if s >= 1:
                 inverse_rms(s - 1)
 
         halves = (FIRST_TILES, SECOND_TILES)
         multiply_rot(LAST - 1)
-        quantize_w(VALUE, 1)
-        quantize_w(VALUE, 0)
+        quantize_w(VALUE)
         transpose_and_add(LAST - 2)
         project(LAST)
         sum_squares(LAST - 2)
-        scale_on_scalar(LAST - 3, ALL_TILES, 0)
-        store(LAST - 3)
+        scale_on_scalar_and_store(LAST - 3)
         inverse_rms(LAST - 2)
 
         for part in halves:

from contextlib import ExitStack

import concourse.mybir as mybir
from concourse.masks import make_identity

L, DIM, H, D = 512, 2048, 16, 128
HALF = D // 2
EPS = 1e-6
FLOPS = 2 * L * DIM * (H * D + 2 * D)

F32 = mybir.dt.float32
BF16 = mybir.dt.bfloat16
U32 = mybir.dt.uint32
U8 = mybir.dt.uint8
E4M3 = mybir.dt.float8_e4m3fn_x4
E5M2 = mybir.dt.float8_e5m2_x4
ACT = mybir.ActivationFunctionType
ALU = mybir.AluOpType

P = 128
PACK = 4
K_PASS = P * PACK
PASSES = DIM // K_PASS
TT = L // P
LAST = H
VALUE = H + 1
RUN = 4
WQ_WIDTHS = [256, 256, 512, 512, 512]
VECTOR_COLS = 108
ALL_TILES = (0, TT)
FIRST_TILES, SECOND_TILES = (0, TT // 2), (TT // 2, TT // 2)


def tile_multiqueryattention_pa_kernel(tc, x, cos, sin, Wq, Wk, Wv, out_0, out_1, out_2):
    nc = tc.nc
    with ExitStack() as ctx:
        keep = ctx.enter_context(tc.tile_pool(name="keep", bufs=1))
        work = ctx.enter_context(tc.tile_pool(name="work", bufs=3))
        outs = ctx.enter_context(tc.tile_pool(name="outs", bufs=10))
        psum = ctx.enter_context(tc.psum_pool(name="psum", bufs=1))
        ctx.enter_context(tc.manual_schedule())

        def product_bank(shape):
            return psum.tile(shape, F32, tag="product", bufs=3, name="product")

        def transpose_bank(shape, dtype):
            return psum.tile(shape, dtype, tag="transposed", bufs=5, name="transposed")

        x_rows = x[0].rearrange("(p t) k -> p t k", t=TT)
        q_rows = out_0[0].rearrange("(p t) h d -> p t h d", t=TT)
        k_rows = out_1[0].rearrange("(p t) d -> p t d", t=TT)
        v_rows = out_2[0].rearrange("(p t) d -> p t d", t=TT)

        def x_pieces(g):
            return [slice(0, TT // 2), slice(TT // 2, TT)] if g == 0 else [slice(0, TT)]

        def load_one_head(name, w_hbm):
            raw = keep.tile([P, PASSES, PACK, D], BF16, name=name)
            nc.sync.dma_start(
                out=raw[:].rearrange("p g j c -> p g (j c)"),
                in_=w_hbm.rearrange("(g p j) c -> p g (j c)", g=PASSES, j=PACK),
            )
            return raw[:]

        cos_raw = keep.tile([P, TT, HALF], BF16, name="cos_raw")
        sin_raw = keep.tile([P, TT, HALF], BF16, name="sin_raw")
        x_raw = [keep.tile([P, TT, K_PASS], BF16, name="x_raw%d" % g) for g in range(PASSES)]
        for g in range(PASSES):
            for toks in x_pieces(g):
                nc.sync.dma_start(out=x_raw[g][:, toks, :], in_=x_rows[:, toks, g * K_PASS : (g + 1) * K_PASS])
            if g == 0:
                nc.sync.dma_start(out=cos_raw[:], in_=cos.rearrange("(p t) o j -> p t (o j)", t=TT))
                nc.sync.dma_start(out=sin_raw[:], in_=sin.rearrange("(p t) o j -> p t (o j)", t=TT))

        w_raw = [load_one_head("wk_raw", Wk)]
        col0 = 0
        for n, width in enumerate(WQ_WIDTHS):
            raw = keep.tile([P, PASSES, PACK, width], BF16, name="wq_raw%d" % n)
            for g in range(PASSES):
                rows = Wq[g * K_PASS : (g + 1) * K_PASS, col0 : col0 + width]
                nc.sync.dma_start(out=raw[:, g, :, :], in_=rows.rearrange("(p j) c -> p j c", j=PACK))
            w_raw.extend(raw[:, :, :, i * D : (i + 1) * D] for i in range(width // D))
            col0 += width
        w_raw.append(load_one_head("wv_raw", Wv))

        ident = keep.tile([P, P], F32, name="ident")
        make_identity(nc, ident[:])
        swap = keep.tile([P, P], F32, name="swap")
        nc.gpsimd.tensor_copy(out=swap[:, 0:HALF], in_=ident[:, HALF:D])
        nc.gpsimd.tensor_copy(out=swap[:, HALF:D], in_=ident[:, 0:HALF])
        ident_bf16 = keep.tile([P, P], BF16, name="ident_bf16")
        make_identity(nc, ident_bf16[:])

        rot_by_token = keep.tile([P, 2, TT, D], BF16, name="rot_by_token")
        rot = keep.tile([P, 2, L], BF16, name="rot")

        def lay_out_rot():
            nc.scalar.activation(out=rot_by_token[:, 1, :, 0:HALF], in_=sin_raw[:], func=ACT.Copy, scale=-1.0)
            nc.scalar.copy(out=rot_by_token[:, 1, :, HALF:D], in_=sin_raw[:])
            nc.scalar.copy(
                out=rot_by_token[:, 0, :, :].rearrange("p t (e j) -> p t e j", e=2),
                in_=cos_raw[:].unsqueeze(2).to_broadcast([P, TT, 2, HALF]),
            )

        def transpose_rot():
            bank = transpose_bank([P, 2, TT, P], BF16)
            for i in range(2):
                for t in range(TT):
                    nc.tensor.transpose(bank[:, i, t, :], rot_by_token[:, i, t, :], ident_bf16[:])
            nc.scalar.copy(out=rot[:], in_=bank[:].rearrange("p i t n -> p i (t n)"))

        x_codes = keep.tile([P, PASSES, L], U32, align_bytes=64, name="x_codes")
        x_scales = keep.tile([P, PASSES, L], U8, align_bytes=64, name="x_scales")
        x_split, x_grouped = {}, {}

        def split_x(g):
            x_split[g] = work.tile([P, TT, 2, P], F32, tag="x_split", name="x_split")
            for toks in x_pieces(g):
                nc.vector.tensor_copy(
                    out=x_split[g][:, toks, :, :],
                    in_=x_raw[g][:, toks, :].bitcast(F32).rearrange("p t (w u) -> p t u w", u=2),
                )

        def transpose_x(g):
            x_grouped[g] = work.tile([P, L * PACK], BF16, align_bytes=64, tag="x_grouped", name="x_grouped")
            words_out = x_grouped[g][:].bitcast(F32).rearrange("p (t r u) -> p t r u", t=TT, u=2)
            for t0 in range(0, TT, 2):
                bank = transpose_bank([P, 2, 2, P], F32)
                for t in range(2):
                    for u in range(2):
                        nc.tensor.transpose(bank[:, t, u, :], x_split[g][:, t0 + t, u, :], ident[:])
                nc.scalar.copy(out=words_out[:, t0 : t0 + 2, :, :], in_=bank[:].rearrange("p t u r -> p t r u"))

        def quantize_x(g):
            nc.vector.quantize_mx(out=x_codes[:, g, :].bitcast(E5M2), scales=x_scales[:, g, :], in_=x_grouped[g][:])

        w_front, w_last, w_codes, w_scales = {}, {}, {}, {}

        def interleave_on_vector(grouped, raw):
            nc.vector.tensor_copy(
                out=grouped.rearrange("p g (c i) j -> p g c j i", i=RUN),
                in_=raw.rearrange("p g j (c i) -> p g c j i", i=RUN),
            )

        def interleave_on_scalar(grouped, raw):
            nc.scalar.copy(out=grouped, in_=raw.rearrange("p g j c -> p g c j"))

        def interleave_on_gpsimd(grouped, raw):
            nc.gpsimd.tensor_copy(out=grouped[:, 0, :, :], in_=raw[:, 0, :, :].rearrange("p j c -> p c j"))

        def interleave_front(h, vector_cols, interleave_third):
            w_front[h] = work.tile([P, PASSES - 1, D, PACK], BF16, align_bytes=64, tag="w_front", name="w_front")
            interleave_on_vector(w_front[h][:, 0:2, 0:vector_cols, :], w_raw[h][:, 0:2, :, 0:vector_cols])
            interleave_third(w_front[h][:, 2:3, :, :], w_raw[h][:, 2:3, :, :])
            if vector_cols < D:
                interleave_on_scalar(w_front[h][:, 0:2, vector_cols:D, :], w_raw[h][:, 0:2, :, vector_cols:D])

        def interleave_last(h, interleave):
            w_last[h] = work.tile([P, 1, D, PACK], BF16, align_bytes=64, tag="w_last", bufs=1, name="w_last")
            interleave(w_last[h][:], w_raw[h][:, PASSES - 1 : PASSES, :, :])

        def quantize_w(h):
            w_codes[h] = work.tile([P, PASSES * D], U32, align_bytes=64, tag="w_codes", bufs=4, name="w_codes")
            w_scales[h] = work.tile([P, PASSES * D], U8, align_bytes=64, tag="w_scales", bufs=4, name="w_scales")
            cut = (PASSES - 1) * D
            for grouped, cols in ((w_front[h], slice(0, cut)), (w_last[h], slice(cut, PASSES * D))):
                nc.vector.quantize_mx(
                    out=w_codes[h][:, cols].bitcast(E4M3),
                    scales=w_scales[h][:, cols],
                    in_=grouped[:].rearrange("p g c j -> p (g c j)"),
                )

        proj, terms, rotated, results, sum_sq, inv_rms, values = {}, {}, {}, {}, {}, {}, {}

        def project(h):
            proj[h] = product_bank([P, L])
            for g in range(PASSES):
                cols = slice(g * D, (g + 1) * D)
                nc.tensor.matmul_mx(
                    out=proj[h][:],
                    lhsT=w_codes[h][:, cols].bitcast(E4M3),
                    lhsT_scale=w_scales[h][:, cols],
                    rhs=x_codes[:, g, :].bitcast(E5M2),
                    rhs_scale=x_scales[:, g, :],
                    start=(g == 0),
                    stop=(g == PASSES - 1),
                )

        def multiply_rot(h, part=ALL_TILES):
            t0, nt = part
            toks = slice(t0 * P, (t0 + nt) * P)
            terms[h, part] = work.tile([P, 2, nt * P], F32, tag="terms", name="terms")
            nc.vector.tensor_tensor(
                out=terms[h, part][:],
                in0=proj[h][:, toks].unsqueeze(1).to_broadcast([P, 2, nt * P]),
                in1=rot[:, :, toks],
                op=ALU.mult,
            )

        def transpose_and_add(h, part=ALL_TILES):
            nt = part[1]
            rotated[h, part] = transpose_bank([P, nt, D], F32)
            for t in range(nt):
                for i, permutation in enumerate((ident, swap)):
                    nc.tensor.matmul(
                        rotated[h, part][:, t, :],
                        lhsT=terms[h, part][:, i, t * P : (t + 1) * P],
                        rhs=permutation[:],
                        start=(i == 0),
                        stop=(i == 1),
                        is_transpose=True,
                    )

        def sum_squares(h, part=ALL_TILES):
            nt = part[1]
            results[h, part] = outs.tile([P, nt, D], F32, tag="result", name="result")
            sum_sq[h, part] = work.tile([P, nt], F32, tag="sum_sq", name="sum_sq")
            for t in range(nt):
                nc.scalar.activation(
                    out=results[h, part][:, t, :],
                    in_=rotated[h, part][:, t, :],
                    func=ACT.Square,
                    accum_out=sum_sq[h, part][:, t : t + 1],
                )

        def inverse_rms(h, part=ALL_TILES):
            inv_rms[h, part] = work.tile([P, part[1]], F32, tag="inv_rms", name="inv_rms")
            nc.scalar.activation(
                out=inv_rms[h, part][:], in_=sum_sq[h, part][:], func=ACT.Abs_reciprocal_sqrt, scale=1.0 / D, bias=EPS
            )

        def store(h, part):
            t0, nt = part
            rows = k_rows if h == 0 else q_rows[:, :, h - 1, :]
            nc.sync.dma_start(out=rows[:, t0 : t0 + nt, :], in_=results[h, part][:])

        def scale_on_scalar_and_store(h):
            for t in range(TT):
                nc.scalar.activation(
                    out=results[h, ALL_TILES][:, t, :],
                    in_=rotated[h, ALL_TILES][:, t, :],
                    func=ACT.Copy,
                    scale=inv_rms[h, ALL_TILES][:, t : t + 1],
                )
            store(h, ALL_TILES)

        def scale_on_vector_and_store(h, part=ALL_TILES):
            nc.vector.tensor_tensor(
                out=results[h, part][:],
                in0=rotated[h, part][:],
                in1=inv_rms[h, part][:].unsqueeze(2).to_broadcast([P, part[1], D]),
                op=ALU.mult,
            )
            store(h, part)

        def project_values(part):
            t0, nt = part
            values[part] = product_bank([P, nt, D])
            for t in range(nt):
                toks = slice((t0 + t) * P, (t0 + t + 1) * P)
                for g in range(PASSES):
                    cols = slice(g * D, (g + 1) * D)
                    nc.tensor.matmul_mx(
                        out=values[part][:, t, :],
                        lhsT=x_codes[:, g, toks].bitcast(E5M2),
                        lhsT_scale=x_scales[:, g, toks],
                        rhs=w_codes[VALUE][:, cols].bitcast(E4M3),
                        rhs_scale=w_scales[VALUE][:, cols],
                        start=(g == 0),
                        stop=(g == PASSES - 1),
                    )

        def store_values(part):
            t0, nt = part
            result = outs.tile([P, nt, D], F32, tag="result", name="result")
            nc.vector.tensor_copy(out=result[:], in_=values[part][:])
            nc.sync.dma_start(out=v_rows[:, t0 : t0 + nt, :], in_=result[:])

        lay_out_rot()
        split_x(0)
        for g in range(PASSES):
            transpose_x(g)
            if g + 1 < PASSES:
                split_x(g + 1)
            if 1 <= g < PASSES - 1:
                quantize_x(g - 1)
        transpose_rot()
        interleave_last(0, interleave_on_vector)
        interleave_front(0, D, interleave_on_vector)
        quantize_x(PASSES - 2)
        quantize_w(0)
        quantize_x(PASSES - 1)
        project(0)
        interleave_last(1, interleave_on_scalar)
        interleave_front(1, VECTOR_COLS, interleave_on_scalar)
        interleave_front(2, VECTOR_COLS, interleave_on_scalar)
        quantize_w(1)
        interleave_last(2, interleave_on_scalar)

        for s in range(LAST - 1):
            multiply_rot(s)
            quantize_w(s + 2)
            interleave_front(s + 3, VECTOR_COLS, interleave_on_scalar)
            interleave_last(s + 3, interleave_on_gpsimd)
            if s >= 1:
                transpose_and_add(s - 1)
            project(s + 1)
            if s >= 1:
                sum_squares(s - 1)
            if s >= 2:
                scale_on_scalar_and_store(s - 2)
            if s >= 1:
                inverse_rms(s - 1)

        halves = (FIRST_TILES, SECOND_TILES)
        multiply_rot(LAST - 1)
        quantize_w(VALUE)
        transpose_and_add(LAST - 2)
        project(LAST)
        sum_squares(LAST - 2)
        scale_on_scalar_and_store(LAST - 3)
        inverse_rms(LAST - 2)

        for part in halves:
            multiply_rot(LAST, part)
        transpose_and_add(LAST - 1)
        project_values(FIRST_TILES)
        for part in halves:
            transpose_and_add(LAST, part)
        project_values(SECOND_TILES)
        sum_squares(LAST - 1)
        scale_on_vector_and_store(LAST - 2)
        inverse_rms(LAST - 1)

        for part in halves:
            sum_squares(LAST, part)
        for part in halves:
            inverse_rms(LAST, part)
        store_values(FIRST_TILES)
        scale_on_vector_and_store(LAST - 1)
        store_values(SECOND_TILES)
        for part in halves:
            scale_on_vector_and_store(LAST, part)
